import numpy as np
import ml_dtypes


def mxq(x, axis, fmt="e4m3"):
    dtype, down = {"e4m3": (ml_dtypes.float8_e4m3fn, 7), "e5m2": (ml_dtypes.float8_e5m2, 14)}[fmt]
    v = np.moveaxis(np.asarray(x, np.float32).astype(ml_dtypes.bfloat16).astype(np.float64), axis, -1)
    blocks = v.reshape(v.shape[:-1] + (-1, 32))
    amax = np.abs(blocks).max(-1, keepdims=True)
    byte = np.maximum(np.where(amax > 0, np.frexp(amax)[1] - 1 + 127, 0) - down, 1)
    scale = np.exp2(byte - 127.0)
    codes = (blocks / scale).astype(np.float32).astype(dtype).astype(np.float64)
    return np.moveaxis((codes * scale).reshape(v.shape), -1, axis)


WIDE = False


def mx_kscale(k):
    if not WIDE:
        return np.ones(k)
    levels = np.array([20, -20, 10, -10, 0])
    a = np.random.permutation(np.resize(levels, k // 512 * 4)).reshape(k // 512, 4)
    idx = np.arange(k)
    return np.exp2(a[idx // 512, idx % 128 // 32])


BF16 = ml_dtypes.bfloat16


def bf(x):
    return np.asarray(x, np.float32).astype(BF16)


def f64(x):
    return np.asarray(x).astype(np.float64)


B, F, G, N, L = 256, 128, 512, 100, 1
S2 = (L + 1) ** 2
C2 = sum((2 * k + 1) ** 2 for k in range(L + 1))


def setup_inputs():
    u = mx_kscale(G)[:, None, None]
    x = np.random.standard_normal((B, F, S2))
    psi = np.random.standard_normal((G, F, S2)) / u
    g = np.random.standard_normal((G, B, C2)) * np.exp2(np.random.randint(-12, 1, (1, B, 1))) * 8.0 * u
    return {"x": bf(x), "psi": bf(psi), "grad_out": bf(g)}


def reference(x, psi, grad_out):
    gq = mxq(f64(grad_out), 0, "e5m2")
    pq = mxq(f64(psi), 0, "e4m3")
    scale = 1.0 / np.sqrt(F)
    gx = np.zeros((B, F, S2))
    c = 0
    for l in range(L + 1):
        s, d = l * l, 2 * l + 1
        a = gq[:, :, c:c + d * d].reshape(G, B, d, d).transpose(1, 2, 3, 0).reshape(B * d, d * G)
        p = pq[:, :, s:s + d].transpose(2, 0, 1).reshape(d * G, F)
        o = scale * (a @ p)
        gx[:, :, s:s + d] = o.reshape(B, d, F).transpose(0, 2, 1)
        c += d * d
    return gx

@@ -1,0 +1,127 @@
+import math
+from contextlib import ExitStack
+
+import concourse.mybir as mybir
+
+BF16 = mybir.dt.bfloat16
+F32 = mybir.dt.float32
+I32 = mybir.dt.int32
+U32 = mybir.dt.uint32
+U8 = mybir.dt.uint8
+E4M3X4 = mybir.dt.float8_e4m3fn_x4
+E5M2X4 = mybir.dt.float8_e5m2_x4
+
+P = 128
+PACK = 4
+B, F, G = 256, 128, 512
+S2 = 4
+C2 = 10
+D1 = 3
+assert G == P * PACK
+
+B_TILE = P
+B_TILES = B // B_TILE
+B_CHUNK = 64
+CHUNKS_PER_TILE = B_TILE // B_CHUNK
+VECTOR_SHARE = 0.5
+C_GROUPS = ((0, 4), (4, 8), (8, 10))
+
+STRIP_STEP = S2
+STRIP_BLOCKS = STRIP_STEP * (S2 - 1) + S2 - 1
+
+FLOPS = 2 * G * F * B * (1 + D1 * D1)
+BYTES = 2 * G * F * S2 + 2 * G * B * C2 + 4 * B * F * S2
+
+
+def regroup(nc, grouped, raw):
+    columns = raw.shape[2]
+    split = int(columns * VECTOR_SHARE)
+    nc.vector.tensor_copy(
+        out=grouped[:, :, :split, :].rearrange("p c n j -> p n j c"),
+        in_=raw[:, :, :split, :].rearrange("p j n c -> p n j c"),
+    )
+    nc.scalar.copy(
+        out=grouped[:, :, split:, :].rearrange("p c n j -> p n j c"),
+        in_=raw[:, :, split:, :].rearrange("p j n c -> p n j c"),
+    )
+
+
+def tile_s2conv_pa_s_kernel(tc, x, psi, grad_out, out):
+    nc = tc.nc
+    with ExitStack() as ctx:
+        keep = ctx.enter_context(tc.tile_pool(name="keep", bufs=1))
+        chunks = ctx.enter_context(tc.tile_pool(name="chunks", bufs=B // B_CHUNK))
+        tiles = ctx.enter_context(tc.tile_pool(name="tiles", bufs=B_TILES))
+        psum = ctx.enter_context(tc.psum_pool(name="psum", bufs=B_TILES))
+
+        psi_raw = keep.tile([P, PACK, F, S2], BF16)
+        nc.sync.dma_start(out=psi_raw[:], in_=psi.rearrange("(p j) f s -> p j f s", j=PACK))
+        grad_rows = grad_out.rearrange("(p j) b c -> p j b c", j=PACK)
+        grad_raws = []
+        for b0 in range(0, B, B_CHUNK):
+            grad_raw = chunks.tile([P, PACK, B_CHUNK, C2], BF16)
+            nc.sync.dma_start(out=grad_raw[:], in_=grad_rows[:, :, b0 : b0 + B_CHUNK, :])
+            grad_raws.append(grad_raw)
+
+        psi_codes = keep.tile([P, STRIP_BLOCKS * F], U32, align_bytes=64)
+        psi_scales = keep.tile([P, STRIP_BLOCKS * F], U8, align_bytes=64)
+        nc.vector.memset(psi_codes[:].bitcast(I32), 0)
+        nc.vector.memset(psi_scales[:].bitcast(I32), 0)
+        psi_grouped = keep.tile([P, S2, F, PACK], BF16, align_bytes=64)
+        regroup(nc, psi_grouped[:], psi_raw[:])
+        for s in range(S2):
+            block = slice(STRIP_STEP * s * F, (STRIP_STEP * s + 1) * F)
+            nc.vector.quantize_mx(
+                out=psi_codes[:, block].bitcast(E4M3X4),
+                scales=psi_scales[:, block],
+                in_=psi_grouped[:, s, :, :].rearrange("p f j -> p (f j)"),
+            )
+
+        sums = []
+        for bt in range(B_TILES):
+            grad_codes = tiles.tile([P, C2, B_TILE], U32, align_bytes=64)
+            grad_scales = tiles.tile([P, C2, B_TILE], U8, align_bytes=64)
+            for half in range(CHUNKS_PER_TILE):
+                grad_raw = grad_raws[bt * CHUNKS_PER_TILE + half]
+                grad_grouped = chunks.tile([P, C2, B_CHUNK, PACK], BF16, align_bytes=64)
+                cols = slice(half * B_CHUNK, (half + 1) * B_CHUNK)
+                for step in range(len(C_GROUPS) + 1):
+                    if step < len(C_GROUPS):
+                        c0, c1 = C_GROUPS[step]
+                        regroup(nc, grad_grouped[:, c0:c1, :, :], grad_raw[:, :, :, c0:c1])
+                    if step > 0:
+                        c0, c1 = C_GROUPS[step - 1]
+                        for c in range(c0, c1):
+                            nc.vector.quantize_mx(
+                                out=grad_codes[:, c, cols].bitcast(E5M2X4),
+                                scales=grad_scales[:, c, cols],
+                                in_=grad_grouped[:, c, :, :].rearrange("p b j -> p (b j)"),
+                            )
+
+            acc = psum.tile([B_TILE, S2 * F], F32)
+            for c in range(C2):
+                if c == 0:
+                    s, place = 0, 0
+                else:
+                    s, place = 1 + (c - 1) % D1, 1 + (c - 1) // D1
+                first = (STRIP_STEP * s - place) * F
+                window = slice(first, first + S2 * F)
+                nc.tensor.matmul_mx(
+                    out=acc[:],
+                    lhsT=grad_codes[:, c, :].bitcast(E5M2X4),
+                    lhsT_scale=grad_scales[:, c, :],
+                    rhs=psi_codes[:, window].bitcast(E4M3X4),
+                    rhs_scale=psi_scales[:, window],
+                    start=(c == 0),
+                    stop=(c == C2 - 1),
+                )
+            sums.append(acc)
+
+        for bt in range(B_TILES):
+            result = tiles.tile([B_TILE, F, S2], F32)
+            nc.vector.tensor_scalar_mul(
+                out=result[:],
+                in0=sums[bt][:].rearrange("b (s f) -> b f s", s=S2),
+                scalar1=1.0 / math.sqrt(F),
+            )
+            nc.sync.dma_start(out=out[bt * B_TILE : (bt + 1) * B_TILE, :, :], in_=result[:])

@@ -49,6 +49,7 @@ def regroup(nc, grouped, raw):
 def tile_s2conv_pa_s_kernel(tc, x, psi, grad_out, out):
     nc = tc.nc
     with ExitStack() as ctx:
+        ctx.enter_context(tc.manual_schedule())
         keep = ctx.enter_context(tc.tile_pool(name="keep", bufs=1))
         chunks = ctx.enter_context(tc.tile_pool(name="chunks", bufs=B // B_CHUNK))
         tiles = ctx.enter_context(tc.tile_pool(name="tiles", bufs=B_TILES))

@@ -23,19 +23,21 @@ B_TILE = P
 B_TILES = B // B_TILE
 B_CHUNK = 64
 CHUNKS_PER_TILE = B_TILE // B_CHUNK
-VECTOR_SHARE = 0.5
-C_GROUPS = ((0, 4), (4, 8), (8, 10))
+PSI_VECTOR_SHARE = 0.625
+GRAD_VECTOR_SHARE = 0.4375
+C_GROUPS = ((0, 2), (2, 6), (6, 10))
 
 STRIP_STEP = S2
-STRIP_BLOCKS = STRIP_STEP * (S2 - 1) + S2 - 1
+STRIP_BLOCKS = STRIP_STEP * S2 + 1
+WARM_PASSES = 10
 
 FLOPS = 2 * G * F * B * (1 + D1 * D1)
 BYTES = 2 * G * F * S2 + 2 * G * B * C2 + 4 * B * F * S2
 
 
-def regroup(nc, grouped, raw):
+def regroup(nc, grouped, raw, vector_share):
     columns = raw.shape[2]
-    split = int(columns * VECTOR_SHARE)
+    split = int(columns * vector_share)
     nc.vector.tensor_copy(
         out=grouped[:, :, :split, :].rearrange("p c n j -> p n j c"),
         in_=raw[:, :, :split, :].rearrange("p j n c -> p n j c"),
@@ -68,8 +70,21 @@ def tile_s2conv_pa_s_kernel(tc, x, psi, grad_out, out):
         psi_scales = keep.tile([P, STRIP_BLOCKS * F], U8, align_bytes=64)
         nc.vector.memset(psi_codes[:].bitcast(I32), 0)
         nc.vector.memset(psi_scales[:].bitcast(I32), 0)
+        zeros = slice((STRIP_BLOCKS - S2) * F, STRIP_BLOCKS * F)
+        zero_block = slice((STRIP_BLOCKS - S2) * F, (STRIP_BLOCKS - S2 + 1) * F)
+        warm_sums = psum.tile([B_TILE, S2 * F], F32)
+        for warm_pass in range(WARM_PASSES):
+            nc.tensor.matmul_mx(
+                out=warm_sums[:],
+                lhsT=psi_codes[:, zero_block].bitcast(E5M2X4),
+                lhsT_scale=psi_scales[:, zero_block],
+                rhs=psi_codes[:, zeros].bitcast(E4M3X4),
+                rhs_scale=psi_scales[:, zeros],
+                start=True,
+                stop=True,
+            )
         psi_grouped = keep.tile([P, S2, F, PACK], BF16, align_bytes=64)
-        regroup(nc, psi_grouped[:], psi_raw[:])
+        regroup(nc, psi_grouped[:], psi_raw[:], PSI_VECTOR_SHARE)
         for s in range(S2):
             block = slice(STRIP_STEP * s * F, (STRIP_STEP * s + 1) * F)
             nc.vector.quantize_mx(
@@ -89,7 +104,12 @@ def tile_s2conv_pa_s_kernel(tc, x, psi, grad_out, out):
                 for step in range(len(C_GROUPS) + 1):
                     if step < len(C_GROUPS):
                         c0, c1 = C_GROUPS[step]
-                        regroup(nc, grad_grouped[:, c0:c1, :, :], grad_raw[:, :, :, c0:c1])
+                        regroup(
+                            nc,
+                            grad_grouped[:, c0:c1, :, :],
+                            grad_raw[:, :, :, c0:c1],
+                            GRAD_VECTOR_SHARE,
+                        )
                     if step > 0:
                         c0, c1 = C_GROUPS[step - 1]
                         for c in range(c0, c1):

@@ -24,28 +24,34 @@ B_TILES = B // B_TILE
 B_CHUNK = 64
 CHUNKS_PER_TILE = B_TILE // B_CHUNK
 PSI_VECTOR_SHARE = 0.625
-GRAD_VECTOR_SHARE = 0.4375
-C_GROUPS = ((0, 2), (2, 6), (6, 10))
+FIRST_CHUNK_VECTOR_SHARE = 0.5
+LAST_CHUNK_VECTOR_SHARE = 0.375
+TILE_GROUPS = (
+    ((0, 2), (2, 6), (6, 10)),
+    ((0, 2), (2, 4), (4, 6), (6, 8), (8, 9), (9, 10)),
+)
+EARLY_GROUPS = (3, 2)
 
 STRIP_STEP = S2
 STRIP_BLOCKS = STRIP_STEP * S2 + 1
-WARM_PASSES = 10
+WARM_PASSES = 14
 
 FLOPS = 2 * G * F * B * (1 + D1 * D1)
 BYTES = 2 * G * F * S2 + 2 * G * B * C2 + 4 * B * F * S2
 
 
+def interleave(engine_copy, grouped, raw):
+    engine_copy(
+        out=grouped.rearrange("p c n j -> p n j c"),
+        in_=raw.rearrange("p j n c -> p n j c"),
+    )
+
+
 def regroup(nc, grouped, raw, vector_share):
     columns = raw.shape[2]
     split = int(columns * vector_share)
-    nc.vector.tensor_copy(
-        out=grouped[:, :, :split, :].rearrange("p c n j -> p n j c"),
-        in_=raw[:, :, :split, :].rearrange("p j n c -> p n j c"),
-    )
-    nc.scalar.copy(
-        out=grouped[:, :, split:, :].rearrange("p c n j -> p n j c"),
-        in_=raw[:, :, split:, :].rearrange("p j n c -> p n j c"),
-    )
+    interleave(nc.vector.tensor_copy, grouped[:, :, :split, :], raw[:, :, :split, :])
+    interleave(nc.scalar.copy, grouped[:, :, split:, :], raw[:, :, split:, :])
 
 
 def tile_s2conv_pa_s_kernel(tc, x, psi, grad_out, out):
@@ -68,8 +74,11 @@ def tile_s2conv_pa_s_kernel(tc, x, psi, grad_out, out):
 
         psi_codes = keep.tile([P, STRIP_BLOCKS * F], U32, align_bytes=64)
         psi_scales = keep.tile([P, STRIP_BLOCKS * F], U8, align_bytes=64)
-        nc.vector.memset(psi_codes[:].bitcast(I32), 0)
-        nc.vector.memset(psi_scales[:].bitcast(I32), 0)
+        codes_words = psi_codes[:].bitcast(I32)
+        scale_words = psi_scales[:].bitcast(I32)
+        tail_start = (STRIP_BLOCKS - S2) * F
+        nc.vector.memset(codes_words[:, tail_start:], 0)
+        nc.vector.memset(scale_words[:, tail_start // 4 :], 0)
         zeros = slice((STRIP_BLOCKS - S2) * F, STRIP_BLOCKS * F)
         zero_block = slice((STRIP_BLOCKS - S2) * F, (STRIP_BLOCKS - S2 + 1) * F)
         warm_sums = psum.tile([B_TILE, S2 * F], F32)
@@ -83,6 +92,13 @@ def tile_s2conv_pa_s_kernel(tc, x, psi, grad_out, out):
                 start=True,
                 stop=True,
             )
+        gaps = (S2 - 1) * STRIP_STEP * F
+        nc.vector.memset(
+            codes_words[:, :gaps].rearrange("p (s n) -> p s n", s=S2 - 1)[:, :, F:], 0
+        )
+        nc.vector.memset(
+            scale_words[:, : gaps // 4].rearrange("p (s n) -> p s n", s=S2 - 1)[:, :, F // 4 :], 0
+        )
         psi_grouped = keep.tile([P, S2, F, PACK], BF16, align_bytes=64)
         regroup(nc, psi_grouped[:], psi_raw[:], PSI_VECTOR_SHARE)
         for s in range(S2):
@@ -93,34 +109,25 @@ def tile_s2conv_pa_s_kernel(tc, x, psi, grad_out, out):
                 in_=psi_grouped[:, s, :, :].rearrange("p f j -> p (f j)"),
             )
 
-        sums = []
+        grouped_tiles, code_tiles, scale_tiles, sums = [], [], [], []
         for bt in range(B_TILES):
+            grad_grouped = tiles.tile([P, C2, B_TILE, PACK], BF16, align_bytes=64)
             grad_codes = tiles.tile([P, C2, B_TILE], U32, align_bytes=64)
             grad_scales = tiles.tile([P, C2, B_TILE], U8, align_bytes=64)
-            for half in range(CHUNKS_PER_TILE):
-                grad_raw = grad_raws[bt * CHUNKS_PER_TILE + half]
-                grad_grouped = chunks.tile([P, C2, B_CHUNK, PACK], BF16, align_bytes=64)
-                cols = slice(half * B_CHUNK, (half + 1) * B_CHUNK)
-                for step in range(len(C_GROUPS) + 1):
-                    if step < len(C_GROUPS):
-                        c0, c1 = C_GROUPS[step]
-                        regroup(
-                            nc,
-                            grad_grouped[:, c0:c1, :, :],
-                            grad_raw[:, :, :, c0:c1],
-                            GRAD_VECTOR_SHARE,
-                        )
-                    if step > 0:
-                        c0, c1 = C_GROUPS[step - 1]
-                        for c in range(c0, c1):
-                            nc.vector.quantize_mx(
-                                out=grad_codes[:, c, cols].bitcast(E5M2X4),
-                                scales=grad_scales[:, c, cols],
-                                in_=grad_grouped[:, c, :, :].rearrange("p b j -> p (b j)"),
-                            )
-
             acc = psum.tile([B_TILE, S2 * F], F32)
-            for c in range(C2):
+            grouped_tiles.append(grad_grouped)
+            code_tiles.append(grad_codes)
+            scale_tiles.append(grad_scales)
+            sums.append(acc)
+
+        def quantise_and_multiply(bt, group):
+            c0, c1 = TILE_GROUPS[bt][group]
+            nc.vector.quantize_mx(
+                out=code_tiles[bt][:, c0:c1, :].rearrange("p c b -> p (c b)").bitcast(E5M2X4),
+                scales=scale_tiles[bt][:, c0:c1, :].rearrange("p c b -> p (c b)"),
+                in_=grouped_tiles[bt][:, c0:c1, :, :].rearrange("p c b j -> p (c b j)"),
+            )
+            for c in range(c0, c1):
                 if c == 0:
                     s, place = 0, 0
                 else:
@@ -128,21 +135,49 @@ def tile_s2conv_pa_s_kernel(tc, x, psi, grad_out, out):
                 first = (STRIP_STEP * s - place) * F
                 window = slice(first, first + S2 * F)
                 nc.tensor.matmul_mx(
-                    out=acc[:],
-                    lhsT=grad_codes[:, c, :].bitcast(E5M2X4),
-                    lhsT_scale=grad_scales[:, c, :],
+                    out=sums[bt][:],
+                    lhsT=code_tiles[bt][:, c, :].bitcast(E5M2X4),
+                    lhsT_scale=scale_tiles[bt][:, c, :],
                     rhs=psi_codes[:, window].bitcast(E4M3X4),
                     rhs_scale=psi_scales[:, window],
                     start=(c == 0),
                     stop=(c == C2 - 1),
                 )
-            sums.append(acc)
+
+        def scale_and_store(bt, engine_mul):
+            result = tiles.tile([B_TILE, F, S2], F32)
+            engine_mul(result[:], sums[bt][:].rearrange("b (s f) -> b f s", s=S2), 1.0 / math.sqrt(F))
+            nc.sync.dma_start(out=out[bt * B_TILE : (bt + 1) * B_TILE, :, :], in_=result[:])
 
         for bt in range(B_TILES):
-            result = tiles.tile([B_TILE, F, S2], F32)
-            nc.vector.tensor_scalar_mul(
-                out=result[:],
-                in0=sums[bt][:].rearrange("b (s f) -> b f s", s=S2),
-                scalar1=1.0 / math.sqrt(F),
-            )
-            nc.sync.dma_start(out=out[bt * B_TILE : (bt + 1) * B_TILE, :, :], in_=result[:])
+            groups = TILE_GROUPS[bt]
+            first_raw, last_raw = grad_raws[bt * CHUNKS_PER_TILE], grad_raws[bt * CHUNKS_PER_TILE + 1]
+            grouped = grouped_tiles[bt]
+            for c0, c1 in groups[: EARLY_GROUPS[bt]]:
+                regroup(
+                    nc,
+                    grouped[:, c0:c1, :B_CHUNK, :],
+                    first_raw[:, :, :, c0:c1],
+                    FIRST_CHUNK_VECTOR_SHARE,
+                )
+            for group in range(len(groups)):
+                c0, c1 = groups[group]
+                if group < EARLY_GROUPS[bt]:
+                    regroup(
+                        nc,
+                        grouped[:, c0:c1, B_CHUNK:, :],
+                        last_raw[:, :, :, c0:c1],
+                        LAST_CHUNK_VECTOR_SHARE,
+                    )
+                else:
+                    interleave(
+                        nc.vector.tensor_copy, grouped[:, c0:c1, :B_CHUNK, :], first_raw[:, :, :, c0:c1]
+                    )
+                    interleave(nc.scalar.copy, grouped[:, c0:c1, B_CHUNK:, :], last_raw[:, :, :, c0:c1])
+                if group > 0:
+                    quantise_and_multiply(bt, group - 1)
+            if bt == B_TILES - 1:
+                for earlier in range(bt):
+                    scale_and_store(earlier, nc.scalar.mul)
+            quantise_and_multiply(bt, len(groups) - 1)
+        scale_and_store(B_TILES - 1, nc.vector.tensor_scalar_mul)

@@ -23,9 +23,9 @@ B_TILE = P
 B_TILES = B // B_TILE
 B_CHUNK = 64
 CHUNKS_PER_TILE = B_TILE // B_CHUNK
-PSI_VECTOR_SHARE = 0.625
-FIRST_CHUNK_VECTOR_SHARE = 0.5
-LAST_CHUNK_VECTOR_SHARE = 0.375
+PSI_VECTOR_SHARE = 0.6875
+FIRST_CHUNK_VECTOR_SHARE = 0.625
+LAST_CHUNK_VECTOR_SHARE = 0.5
 TILE_GROUPS = (
     ((0, 2), (2, 6), (6, 10)),
     ((0, 2), (2, 4), (4, 6), (6, 8), (8, 9), (9, 10)),

@@ -34,7 +34,8 @@ EARLY_GROUPS = (3, 2)
 
 STRIP_STEP = S2
 STRIP_BLOCKS = STRIP_STEP * S2 + 1
-WARM_PASSES = 14
+WARM_PASSES = 8
+BRIDGE_PASSES = 6
 
 FLOPS = 2 * G * F * B * (1 + D1 * D1)
 BYTES = 2 * G * F * S2 + 2 * G * B * C2 + 4 * B * F * S2
@@ -107,6 +108,17 @@ def tile_s2conv_pa_s_kernel(tc, x, psi, grad_out, out):
                 out=psi_codes[:, block].bitcast(E4M3X4),
                 scales=psi_scales[:, block],
                 in_=psi_grouped[:, s, :, :].rearrange("p f j -> p (f j)"),
+            )
+        bridge = slice((STRIP_BLOCKS - S2 - 1) * F, (STRIP_BLOCKS - 1) * F)
+        for bridge_pass in range(BRIDGE_PASSES):
+            nc.tensor.matmul_mx(
+                out=warm_sums[:],
+                lhsT=psi_codes[:, zero_block].bitcast(E5M2X4),
+                lhsT_scale=psi_scales[:, zero_block],
+                rhs=psi_codes[:, bridge].bitcast(E4M3X4),
+                rhs_scale=psi_scales[:, bridge],
+                start=True,
+                stop=True,
             )
 
         grouped_tiles, code_tiles, scale_tiles, sums = [], [], [], []

@@ -132,13 +132,26 @@ def tile_s2conv_pa_s_kernel(tc, x, psi, grad_out, out):
             scale_tiles.append(grad_scales)
             sums.append(acc)
 
-        def quantise_and_multiply(bt, group):
+        def quantise_half(bt, group, half):
+            c0, c1 = TILE_GROUPS[bt][group]
+            cols = slice(half * B_CHUNK, (half + 1) * B_CHUNK)
+            for c in range(c0, c1):
+                nc.vector.quantize_mx(
+                    out=code_tiles[bt][:, c, cols].bitcast(E5M2X4),
+                    scales=scale_tiles[bt][:, c, cols],
+                    in_=grouped_tiles[bt][:, c, cols, :].rearrange("p b j -> p (b j)"),
+                )
+
+        def quantise_whole(bt, group):
             c0, c1 = TILE_GROUPS[bt][group]
             nc.vector.quantize_mx(
                 out=code_tiles[bt][:, c0:c1, :].rearrange("p c b -> p (c b)").bitcast(E5M2X4),
                 scales=scale_tiles[bt][:, c0:c1, :].rearrange("p c b -> p (c b)"),
                 in_=grouped_tiles[bt][:, c0:c1, :, :].rearrange("p c b j -> p (c b j)"),
             )
+
+        def multiply(bt, group):
+            c0, c1 = TILE_GROUPS[bt][group]
             for c in range(c0, c1):
                 if c == 0:
                     s, place = 0, 0
@@ -156,6 +169,13 @@ def tile_s2conv_pa_s_kernel(tc, x, psi, grad_out, out):
                     stop=(c == C2 - 1),
                 )
 
+        def finish(bt, group):
+            if group < EARLY_GROUPS[bt]:
+                quantise_half(bt, group, 1)
+            else:
+                quantise_whole(bt, group)
+            multiply(bt, group)
+
         def scale_and_store(bt, engine_mul):
             result = tiles.tile([B_TILE, F, S2], F32)
             engine_mul(result[:], sums[bt][:].rearrange("b (s f) -> b f s", s=S2), 1.0 / math.sqrt(F))
@@ -165,13 +185,17 @@ def tile_s2conv_pa_s_kernel(tc, x, psi, grad_out, out):
             groups = TILE_GROUPS[bt]
             first_raw, last_raw = grad_raws[bt * CHUNKS_PER_TILE], grad_raws[bt * CHUNKS_PER_TILE + 1]
             grouped = grouped_tiles[bt]
-            for c0, c1 in groups[: EARLY_GROUPS[bt]]:
+            for group in range(EARLY_GROUPS[bt]):
+                c0, c1 = groups[group]
                 regroup(
                     nc,
                     grouped[:, c0:c1, :B_CHUNK, :],
                     first_raw[:, :, :, c0:c1],
                     FIRST_CHUNK_VECTOR_SHARE,
                 )
+                if group > 0:
+                    quantise_half(bt, group - 1, 0)
+            quantise_half(bt, EARLY_GROUPS[bt] - 1, 0)
             for group in range(len(groups)):
                 c0, c1 = groups[group]
                 if group < EARLY_GROUPS[bt]:
@@ -187,9 +211,9 @@ def tile_s2conv_pa_s_kernel(tc, x, psi, grad_out, out):
                     )
                     interleave(nc.scalar.copy, grouped[:, c0:c1, B_CHUNK:, :], last_raw[:, :, :, c0:c1])
                 if group > 0:
-                    quantise_and_multiply(bt, group - 1)
+                    finish(bt, group - 1)
             if bt == B_TILES - 1:
                 for earlier in range(bt):
                     scale_and_store(earlier, nc.scalar.mul)
-            quantise_and_multiply(bt, len(groups) - 1)
+            finish(bt, len(groups) - 1)
         scale_and_store(B_TILES - 1, nc.vector.tensor_scalar_mul)

@@ -28,7 +28,7 @@ FIRST_CHUNK_VECTOR_SHARE = 0.625
 LAST_CHUNK_VECTOR_SHARE = 0.5
 TILE_GROUPS = (
     ((0, 2), (2, 6), (6, 10)),
-    ((0, 2), (2, 4), (4, 6), (6, 8), (8, 9), (9, 10)),
+    ((0, 2), (2, 4), (4, 6), (6, 8), (8, 10)),
 )
 EARLY_GROUPS = (3, 2)
 
@@ -195,7 +195,6 @@ def tile_s2conv_pa_s_kernel(tc, x, psi, grad_out, out):
                 )
                 if group > 0:
                     quantise_half(bt, group - 1, 0)
-            quantise_half(bt, EARLY_GROUPS[bt] - 1, 0)
             for group in range(len(groups)):
                 c0, c1 = groups[group]
                 if group < EARLY_GROUPS[bt]:
@@ -212,6 +211,8 @@ def tile_s2conv_pa_s_kernel(tc, x, psi, grad_out, out):
                     interleave(nc.scalar.copy, grouped[:, c0:c1, B_CHUNK:, :], last_raw[:, :, :, c0:c1])
                 if group > 0:
                     finish(bt, group - 1)
+                if group == 1:
+                    quantise_half(bt, EARLY_GROUPS[bt] - 1, 0)
             if bt == B_TILES - 1:
                 for earlier in range(bt):
                     scale_and_store(earlier, nc.scalar.mul)

@@ -26,11 +26,13 @@ CHUNKS_PER_TILE = B_TILE // B_CHUNK
 PSI_VECTOR_SHARE = 0.6875
 FIRST_CHUNK_VECTOR_SHARE = 0.625
 LAST_CHUNK_VECTOR_SHARE = 0.5
+DEFERRED_VECTOR_SHARE = 0.25
 TILE_GROUPS = (
     ((0, 2), (2, 6), (6, 10)),
     ((0, 2), (2, 4), (4, 6), (6, 8), (8, 10)),
 )
 EARLY_GROUPS = (3, 2)
+DEFER_FROM = (2, 1)
 
 STRIP_STEP = S2
 STRIP_BLOCKS = STRIP_STEP * S2 + 1
@@ -191,9 +193,9 @@ def tile_s2conv_pa_s_kernel(tc, x, psi, grad_out, out):
                     nc,
                     grouped[:, c0:c1, :B_CHUNK, :],
                     first_raw[:, :, :, c0:c1],
-                    FIRST_CHUNK_VECTOR_SHARE,
+                    FIRST_CHUNK_VECTOR_SHARE if group < DEFER_FROM[bt] else DEFERRED_VECTOR_SHARE,
                 )
-                if group > 0:
+                if 0 < group <= DEFER_FROM[bt]:
                     quantise_half(bt, group - 1, 0)
             for group in range(len(groups)):
                 c0, c1 = groups[group]
@@ -211,8 +213,8 @@ def tile_s2conv_pa_s_kernel(tc, x, psi, grad_out, out):
                     interleave(nc.scalar.copy, grouped[:, c0:c1, B_CHUNK:, :], last_raw[:, :, :, c0:c1])
                 if group > 0:
                     finish(bt, group - 1)
-                if group == 1:
-                    quantise_half(bt, EARLY_GROUPS[bt] - 1, 0)
+                if DEFER_FROM[bt] <= group < EARLY_GROUPS[bt]:
+                    quantise_half(bt, group, 0)
             if bt == B_TILES - 1:
                 for earlier in range(bt):
                     scale_and_store(earlier, nc.scalar.mul)

@@ -38,6 +38,7 @@ STRIP_STEP = S2
 STRIP_BLOCKS = STRIP_STEP * S2 + 1
 WARM_PASSES = 8
 BRIDGE_PASSES = 6
+FINAL_FEATURES = 64
 
 FLOPS = 2 * G * F * B * (1 + D1 * D1)
 BYTES = 2 * G * F * S2 + 2 * G * B * C2 + 4 * B * F * S2
@@ -219,4 +220,12 @@ def tile_s2conv_pa_s_kernel(tc, x, psi, grad_out, out):
                 for earlier in range(bt):
                     scale_and_store(earlier, nc.scalar.mul)
             finish(bt, len(groups) - 1)
-        scale_and_store(B_TILES - 1, nc.vector.tensor_scalar_mul)
+        last_sums = sums[B_TILES - 1][:].rearrange("b (s f) -> b f s", s=S2)
+        last_out = out[(B_TILES - 1) * B_TILE :, :, :]
+        result = tiles.tile([B_TILE, F, S2], F32)
+        for f0 in range(0, F, FINAL_FEATURES):
+            piece = slice(f0, f0 + FINAL_FEATURES)
+            nc.vector.tensor_scalar_mul(
+                result[:, piece, :], last_sums[:, piece, :], 1.0 / math.sqrt(F)
+            )
+            nc.sync.dma_start(out=last_out[:, piece, :], in_=result[:, piece, :])

@@ -26,19 +26,20 @@ CHUNKS_PER_TILE = B_TILE // B_CHUNK
 PSI_VECTOR_SHARE = 0.6875
 FIRST_CHUNK_VECTOR_SHARE = 0.625
 LAST_CHUNK_VECTOR_SHARE = 0.5
+OPENING_VECTOR_SHARE = 0.75
 DEFERRED_VECTOR_SHARE = 0.25
 TILE_GROUPS = (
     ((0, 2), (2, 6), (6, 10)),
     ((0, 2), (2, 4), (4, 6), (6, 8), (8, 10)),
 )
 EARLY_GROUPS = (3, 2)
-DEFER_FROM = (2, 1)
+DEFER_FROM = (2, 2)
 
 STRIP_STEP = S2
 STRIP_BLOCKS = STRIP_STEP * S2 + 1
 WARM_PASSES = 8
 BRIDGE_PASSES = 6
-FINAL_FEATURES = 64
+FINAL_FEATURES = 32
 
 FLOPS = 2 * G * F * B * (1 + D1 * D1)
 BYTES = 2 * G * F * S2 + 2 * G * B * C2 + 4 * B * F * S2
@@ -188,14 +189,17 @@ def tile_s2conv_pa_s_kernel(tc, x, psi, grad_out, out):
             groups = TILE_GROUPS[bt]
             first_raw, last_raw = grad_raws[bt * CHUNKS_PER_TILE], grad_raws[bt * CHUNKS_PER_TILE + 1]
             grouped = grouped_tiles[bt]
-            for group in range(EARLY_GROUPS[bt]):
-                c0, c1 = groups[group]
-                regroup(
-                    nc,
-                    grouped[:, c0:c1, :B_CHUNK, :],
-                    first_raw[:, :, :, c0:c1],
-                    FIRST_CHUNK_VECTOR_SHARE if group < DEFER_FROM[bt] else DEFERRED_VECTOR_SHARE,
-                )
+            for group in range(EARLY_GROUPS[bt] + 1):
+                if group < EARLY_GROUPS[bt]:
+                    c0, c1 = groups[group]
+                    regroup(
+                        nc,
+                        grouped[:, c0:c1, :B_CHUNK, :],
+                        first_raw[:, :, :, c0:c1],
+                        FIRST_CHUNK_VECTOR_SHARE
+                        if group < DEFER_FROM[bt]
+                        else DEFERRED_VECTOR_SHARE,
+                    )
                 if 0 < group <= DEFER_FROM[bt]:
                     quantise_half(bt, group - 1, 0)
             for group in range(len(groups)):
@@ -205,7 +209,7 @@ def tile_s2conv_pa_s_kernel(tc, x, psi, grad_out, out):
                         nc,
                         grouped[:, c0:c1, B_CHUNK:, :],
                         last_raw[:, :, :, c0:c1],
-                        LAST_CHUNK_VECTOR_SHARE,
+                        OPENING_VECTOR_SHARE if group == 0 else LAST_CHUNK_VECTOR_SHARE,
                     )
                 else:
                     interleave(

@@ -39,7 +39,7 @@ STRIP_STEP = S2
 STRIP_BLOCKS = STRIP_STEP * S2 + 1
 WARM_PASSES = 8
 BRIDGE_PASSES = 6
-FINAL_FEATURES = 32
+FINAL_FEATURES = 64
 
 FLOPS = 2 * G * F * B * (1 + D1 * D1)
 BYTES = 2 * G * F * S2 + 2 * G * B * C2 + 4 * B * F * S2

@@ -23,6 +23,8 @@ B_TILE = P
 B_TILES = B // B_TILE
 B_CHUNK = 64
 CHUNKS_PER_TILE = B_TILE // B_CHUNK
+LOAD_WIDTHS = (64, 64, 80, 48)
+assert sum(LOAD_WIDTHS) == B
 PSI_VECTOR_SHARE = 0.6875
 FIRST_CHUNK_VECTOR_SHARE = 0.625
 LAST_CHUNK_VECTOR_SHARE = 0.5
@@ -54,7 +56,7 @@ def interleave(engine_copy, grouped, raw):
 
 def regroup(nc, grouped, raw, vector_share):
     columns = raw.shape[2]
-    split = int(columns * vector_share)
+    split = 2 * round(columns * vector_share / 2)
     interleave(nc.vector.tensor_copy, grouped[:, :, :split, :], raw[:, :, :split, :])
     interleave(nc.scalar.copy, grouped[:, :, split:, :], raw[:, :, split:, :])
 
@@ -64,7 +66,7 @@ def tile_s2conv_pa_s_kernel(tc, x, psi, grad_out, out):
     with ExitStack() as ctx:
         ctx.enter_context(tc.manual_schedule())
         keep = ctx.enter_context(tc.tile_pool(name="keep", bufs=1))
-        chunks = ctx.enter_context(tc.tile_pool(name="chunks", bufs=B // B_CHUNK))
+        chunks = ctx.enter_context(tc.tile_pool(name="chunks", bufs=1))
         tiles = ctx.enter_context(tc.tile_pool(name="tiles", bufs=B_TILES))
         psum = ctx.enter_context(tc.psum_pool(name="psum", bufs=B_TILES))
 
@@ -72,10 +74,12 @@ def tile_s2conv_pa_s_kernel(tc, x, psi, grad_out, out):
         nc.sync.dma_start(out=psi_raw[:], in_=psi.rearrange("(p j) f s -> p j f s", j=PACK))
         grad_rows = grad_out.rearrange("(p j) b c -> p j b c", j=PACK)
         grad_raws = []
-        for b0 in range(0, B, B_CHUNK):
-            grad_raw = chunks.tile([P, PACK, B_CHUNK, C2], BF16)
-            nc.sync.dma_start(out=grad_raw[:], in_=grad_rows[:, :, b0 : b0 + B_CHUNK, :])
+        b0 = 0
+        for load, width in enumerate(LOAD_WIDTHS):
+            grad_raw = chunks.tile([P, PACK, width, C2], BF16, name="grad_raw%d" % load)
+            nc.sync.dma_start(out=grad_raw[:], in_=grad_rows[:, :, b0 : b0 + width, :])
             grad_raws.append(grad_raw)
+            b0 += width
 
         psi_codes = keep.tile([P, STRIP_BLOCKS * F], U32, align_bytes=64)
         psi_scales = keep.tile([P, STRIP_BLOCKS * F], U8, align_bytes=64)
@@ -189,12 +193,13 @@ def tile_s2conv_pa_s_kernel(tc, x, psi, grad_out, out):
             groups = TILE_GROUPS[bt]
             first_raw, last_raw = grad_raws[bt * CHUNKS_PER_TILE], grad_raws[bt * CHUNKS_PER_TILE + 1]
             grouped = grouped_tiles[bt]
+            cut = LOAD_WIDTHS[bt * CHUNKS_PER_TILE]
             for group in range(EARLY_GROUPS[bt] + 1):
                 if group < EARLY_GROUPS[bt]:
                     c0, c1 = groups[group]
                     regroup(
                         nc,
-                        grouped[:, c0:c1, :B_CHUNK, :],
+                        grouped[:, c0:c1, :cut, :],
                         first_raw[:, :, :, c0:c1],
                         FIRST_CHUNK_VECTOR_SHARE
                         if group < DEFER_FROM[bt]
@@ -207,15 +212,23 @@ def tile_s2conv_pa_s_kernel(tc, x, psi, grad_out, out):
                 if group < EARLY_GROUPS[bt]:
                     regroup(
                         nc,
-                        grouped[:, c0:c1, B_CHUNK:, :],
+                        grouped[:, c0:c1, cut:, :],
                         last_raw[:, :, :, c0:c1],
                         OPENING_VECTOR_SHARE if group == 0 else LAST_CHUNK_VECTOR_SHARE,
                     )
                 else:
                     interleave(
-                        nc.vector.tensor_copy, grouped[:, c0:c1, :B_CHUNK, :], first_raw[:, :, :, c0:c1]
+                        nc.vector.tensor_copy,
+                        grouped[:, c0:c1, :B_CHUNK, :],
+                        first_raw[:, :, :B_CHUNK, c0:c1],
                     )
-                    interleave(nc.scalar.copy, grouped[:, c0:c1, B_CHUNK:, :], last_raw[:, :, :, c0:c1])
+                    if cut > B_CHUNK:
+                        interleave(
+                            nc.scalar.copy,
+                            grouped[:, c0:c1, B_CHUNK:cut, :],
+                            first_raw[:, :, B_CHUNK:, c0:c1],
+                        )
+                    interleave(nc.scalar.copy, grouped[:, c0:c1, cut:, :], last_raw[:, :, :, c0:c1])
                 if group > 0:
                     finish(bt, group - 1)
                 if DEFER_FROM[bt] <= group < EARLY_GROUPS[bt]:

import math
from contextlib import ExitStack

import concourse.mybir as mybir

BF16 = mybir.dt.bfloat16
F32 = mybir.dt.float32
I32 = mybir.dt.int32
U32 = mybir.dt.uint32
U8 = mybir.dt.uint8
E4M3X4 = mybir.dt.float8_e4m3fn_x4
E5M2X4 = mybir.dt.float8_e5m2_x4

P = 128
PACK = 4
B, F, G = 256, 128, 512
S2 = 4
C2 = 10
D1 = 3
assert G == P * PACK

B_TILE = P
B_TILES = B // B_TILE
B_CHUNK = 64
CHUNKS_PER_TILE = B_TILE // B_CHUNK
LOAD_WIDTHS = (64, 64, 80, 48)
assert sum(LOAD_WIDTHS) == B
PSI_VECTOR_SHARE = 0.6875
FIRST_CHUNK_VECTOR_SHARE = 0.625
LAST_CHUNK_VECTOR_SHARE = 0.5
OPENING_VECTOR_SHARE = 0.75
DEFERRED_VECTOR_SHARE = 0.25
TILE_GROUPS = (
    ((0, 2), (2, 6), (6, 10)),
    ((0, 2), (2, 4), (4, 6), (6, 8), (8, 10)),
)
EARLY_GROUPS = (3, 2)
DEFER_FROM = (2, 2)

STRIP_STEP = S2
STRIP_BLOCKS = STRIP_STEP * S2 + 1
WARM_PASSES = 8
BRIDGE_PASSES = 6
FINAL_FEATURES = 64

FLOPS = 2 * G * F * B * (1 + D1 * D1)
BYTES = 2 * G * F * S2 + 2 * G * B * C2 + 4 * B * F * S2


def interleave(engine_copy, grouped, raw):
    engine_copy(
        out=grouped.rearrange("p c n j -> p n j c"),
        in_=raw.rearrange("p j n c -> p n j c"),
    )


def regroup(nc, grouped, raw, vector_share):
    columns = raw.shape[2]
    split = 2 * round(columns * vector_share / 2)
    interleave(nc.vector.tensor_copy, grouped[:, :, :split, :], raw[:, :, :split, :])
    interleave(nc.scalar.copy, grouped[:, :, split:, :], raw[:, :, split:, :])


def tile_s2conv_pa_s_kernel(tc, x, psi, grad_out, out):
    nc = tc.nc
    with ExitStack() as ctx:
        ctx.enter_context(tc.manual_schedule())
        keep = ctx.enter_context(tc.tile_pool(name="keep", bufs=1))
        chunks = ctx.enter_context(tc.tile_pool(name="chunks", bufs=1))
        tiles = ctx.enter_context(tc.tile_pool(name="tiles", bufs=B_TILES))
        psum = ctx.enter_context(tc.psum_pool(name="psum", bufs=B_TILES))

        psi_raw = keep.tile([P, PACK, F, S2], BF16)
        nc.sync.dma_start(out=psi_raw[:], in_=psi.rearrange("(p j) f s -> p j f s", j=PACK))
        grad_rows = grad_out.rearrange("(p j) b c -> p j b c", j=PACK)
        grad_raws = []
        b0 = 0
        for load, width in enumerate(LOAD_WIDTHS):
            grad_raw = chunks.tile([P, PACK, width, C2], BF16, name="grad_raw%d" % load)
            nc.sync.dma_start(out=grad_raw[:], in_=grad_rows[:, :, b0 : b0 + width, :])
            grad_raws.append(grad_raw)
            b0 += width

        psi_codes = keep.tile([P, STRIP_BLOCKS * F], U32, align_bytes=64)
        psi_scales = keep.tile([P, STRIP_BLOCKS * F], U8, align_bytes=64)
        codes_words = psi_codes[:].bitcast(I32)
        scale_words = psi_scales[:].bitcast(I32)
        tail_start = (STRIP_BLOCKS - S2) * F
        nc.vector.memset(codes_words[:, tail_start:], 0)
        nc.vector.memset(scale_words[:, tail_start // 4 :], 0)
        zeros = slice((STRIP_BLOCKS - S2) * F, STRIP_BLOCKS * F)
        zero_block = slice((STRIP_BLOCKS - S2) * F, (STRIP_BLOCKS - S2 + 1) * F)
        warm_sums = psum.tile([B_TILE, S2 * F], F32)
        for warm_pass in range(WARM_PASSES):
            nc.tensor.matmul_mx(
                out=warm_sums[:],
                lhsT=psi_codes[:, zero_block].bitcast(E5M2X4),
                lhsT_scale=psi_scales[:, zero_block],
                rhs=psi_codes[:, zeros].bitcast(E4M3X4),
                rhs_scale=psi_scales[:, zeros],
                start=True,
                stop=True,
            )
        gaps = (S2 - 1) * STRIP_STEP * F
        nc.vector.memset(
            codes_words[:, :gaps].rearrange("p (s n) -> p s n", s=S2 - 1)[:, :, F:], 0
        )
        nc.vector.memset(
            scale_words[:, : gaps // 4].rearrange("p (s n) -> p s n", s=S2 - 1)[:, :, F // 4 :], 0
        )
        psi_grouped = keep.tile([P, S2, F, PACK], BF16, align_bytes=64)
        regroup(nc, psi_grouped[:], psi_raw[:], PSI_VECTOR_SHARE)
        for s in range(S2):
            block = slice(STRIP_STEP * s * F, (STRIP_STEP * s + 1) * F)
            nc.vector.quantize_mx(
                out=psi_codes[:, block].bitcast(E4M3X4),
                scales=psi_scales[:, block],
                in_=psi_grouped[:, s, :, :].rearrange("p f j -> p (f j)"),
            )
        bridge = slice((STRIP_BLOCKS - S2 - 1) * F, (STRIP_BLOCKS - 1) * F)
        for bridge_pass in range(BRIDGE_PASSES):
            nc.tensor.matmul_mx(
                out=warm_sums[:],
                lhsT=psi_codes[:, zero_block].bitcast(E5M2X4),
                lhsT_scale=psi_scales[:, zero_block],
                rhs=psi_codes[:, bridge].bitcast(E4M3X4),
                rhs_scale=psi_scales[:, bridge],
                start=True,
                stop=True,
            )

        grouped_tiles, code_tiles, scale_tiles, sums = [], [], [], []
        for bt in range(B_TILES):
            grad_grouped = tiles.tile([P, C2, B_TILE, PACK], BF16, align_bytes=64)
            grad_codes = tiles.tile([P, C2, B_TILE], U32, align_bytes=64)
            grad_scales = tiles.tile([P, C2, B_TILE], U8, align_bytes=64)
            acc = psum.tile([B_TILE, S2 * F], F32)
            grouped_tiles.append(grad_grouped)
            code_tiles.append(grad_codes)
            scale_tiles.append(grad_scales)
            sums.append(acc)

        def quantise_half(bt, group, half):
            c0, c1 = TILE_GROUPS[bt][group]
            cols = slice(half * B_CHUNK, (half + 1) * B_CHUNK)
            for c in range(c0, c1):
                nc.vector.quantize_mx(
                    out=code_tiles[bt][:, c, cols].bitcast(E5M2X4),
                    scales=scale_tiles[bt][:, c, cols],
                    in_=grouped_tiles[bt][:, c, cols, :].rearrange("p b j -> p (b j)"),
                )

        def quantise_whole(bt, group):
            c0, c1 = TILE_GROUPS[bt][group]
            nc.vector.quantize_mx(
                out=code_tiles[bt][:, c0:c1, :].rearrange("p c b -> p (c b)").bitcast(E5M2X4),
                scales=scale_tiles[bt][:, c0:c1, :].rearrange("p c b -> p (c b)"),
                in_=grouped_tiles[bt][:, c0:c1, :, :].rearrange("p c b j -> p (c b j)"),
            )

        def multiply(bt, group):
            c0, c1 = TILE_GROUPS[bt][group]
            for c in range(c0, c1):
                if c == 0:
                    s, place = 0, 0
                else:
                    s, place = 1 + (c - 1) % D1, 1 + (c - 1) // D1
                first = (STRIP_STEP * s - place) * F
                window = slice(first, first + S2 * F)
                nc.tensor.matmul_mx(
                    out=sums[bt][:],
                    lhsT=code_tiles[bt][:, c, :].bitcast(E5M2X4),
                    lhsT_scale=scale_tiles[bt][:, c, :],
                    rhs=psi_codes[:, window].bitcast(E4M3X4),
                    rhs_scale=psi_scales[:, window],
                    start=(c == 0),
                    stop=(c == C2 - 1),
                )

        def finish(bt, group):
            if group < EARLY_GROUPS[bt]:
                quantise_half(bt, group, 1)
            else:
                quantise_whole(bt, group)
            multiply(bt, group)

        def scale_and_store(bt, engine_mul):
            result = tiles.tile([B_TILE, F, S2], F32)
            engine_mul(result[:], sums[bt][:].rearrange("b (s f) -> b f s", s=S2), 1.0 / math.sqrt(F))
            nc.sync.dma_start(out=out[bt * B_TILE : (bt + 1) * B_TILE, :, :], in_=result[:])

        for bt in range(B_TILES):
            groups = TILE_GROUPS[bt]
            first_raw, last_raw = grad_raws[bt * CHUNKS_PER_TILE], grad_raws[bt * CHUNKS_PER_TILE + 1]
            grouped = grouped_tiles[bt]
            cut = LOAD_WIDTHS[bt * CHUNKS_PER_TILE]
            for group in range(EARLY_GROUPS[bt] + 1):
                if group < EARLY_GROUPS[bt]:
                    c0, c1 = groups[group]
                    regroup(
                        nc,
                        grouped[:, c0:c1, :cut, :],
                        first_raw[:, :, :, c0:c1],
                        FIRST_CHUNK_VECTOR_SHARE
                        if group < DEFER_FROM[bt]
                        else DEFERRED_VECTOR_SHARE,
                    )
                if 0 < group <= DEFER_FROM[bt]:
                    quantise_half(bt, group - 1, 0)
            for group in range(len(groups)):
                c0, c1 = groups[group]
                if group < EARLY_GROUPS[bt]:
                    regroup(
                        nc,
                        grouped[:, c0:c1, cut:, :],
                        last_raw[:, :, :, c0:c1],
                        OPENING_VECTOR_SHARE if group == 0 else LAST_CHUNK_VECTOR_SHARE,
                    )
                else:
                    interleave(
                        nc.vector.tensor_copy,
                        grouped[:, c0:c1, :B_CHUNK, :],
                        first_raw[:, :, :B_CHUNK, c0:c1],
                    )
                    if cut > B_CHUNK:
                        interleave(
                            nc.scalar.copy,
                            grouped[:, c0:c1, B_CHUNK:cut, :],
                            first_raw[:, :, B_CHUNK:, c0:c1],
                        )
                    interleave(nc.scalar.copy, grouped[:, c0:c1, cut:, :], last_raw[:, :, :, c0:c1])
                if group > 0:
                    finish(bt, group - 1)
                if DEFER_FROM[bt] <= group < EARLY_GROUPS[bt]:
                    quantise_half(bt, group, 0)
            if bt == B_TILES - 1:
                for earlier in range(bt):
                    scale_and_store(earlier, nc.scalar.mul)
            finish(bt, len(groups) - 1)
        last_sums = sums[B_TILES - 1][:].rearrange("b (s f) -> b f s", s=S2)
        last_out = out[(B_TILES - 1) * B_TILE :, :, :]
        result = tiles.tile([B_TILE, F, S2], F32)
        for f0 in range(0, F, FINAL_FEATURES):
            piece = slice(f0, f0 + FINAL_FEATURES)
            nc.vector.tensor_scalar_mul(
                result[:, piece, :], last_sums[:, piece, :], 1.0 / math.sqrt(F)
            )
            nc.sync.dma_start(out=last_out[:, piece, :], in_=result[:, piece, :])
